import numpy as np
import ml_dtypes


def mxq(x, axis, fmt="e4m3"):
    dtype, down = {"e4m3": (ml_dtypes.float8_e4m3fn, 7), "e5m2": (ml_dtypes.float8_e5m2, 14)}[fmt]
    v = np.moveaxis(np.asarray(x, np.float32).astype(ml_dtypes.bfloat16).astype(np.float64), axis, -1)
    blocks = v.reshape(v.shape[:-1] + (-1, 32))
    amax = np.abs(blocks).max(-1, keepdims=True)
    byte = np.maximum(np.where(amax > 0, np.frexp(amax)[1] - 1 + 127, 0) - down, 1)
    scale = np.exp2(byte - 127.0)
    codes = (blocks / scale).astype(np.float32).astype(dtype).astype(np.float64)
    return np.moveaxis((codes * scale).reshape(v.shape), -1, axis)


WIDE = False


def mx_kscale(k):
    if not WIDE:
        return np.ones(k)
    levels = np.array([10, -10, 5, -5, 0])
    if k % 512:
        return np.exp2(np.random.permutation(np.resize(levels, k // 32))).repeat(32)
    a = np.empty((k // 512, 16))
    for p in range(k // 512):
        a[p, :8] = np.random.permutation(np.resize(levels, 8))
        for g in range(8):
            far = levels[np.abs(levels - a[p, g]) >= 10]
            a[p, g + 8] = far[np.random.randint(len(far))]
    return np.exp2(a.ravel()).repeat(32)


BF16 = ml_dtypes.bfloat16


def bf(x):
    return np.asarray(x, np.float32).astype(BF16)


def f64(x):
    return np.asarray(x).astype(np.float64)


B, F, H, C = 4096, 1024, 128, 10
EPS = 4.0 / 30.0
P_KEEP = 0.95


def setup_inputs():
    s = mx_kscale(F)
    ns = EPS / (6.0 * np.sqrt(H))
    return {"x1": bf(np.random.standard_normal((B, F)) * s),
            "x2": bf(np.random.standard_normal((B, F)) * s),
            "W1": bf(np.random.standard_normal((F, H)) / np.sqrt(F) / s[:, None]),
            "b1": bf(np.random.standard_normal(H) * 0.3),
            "W2": bf(np.random.standard_normal((F, H)) / np.sqrt(F) / s[:, None]),
            "b2": bf(np.random.standard_normal(H) * 0.3),
            "noise_std": bf(np.random.laplace(size=(B, H)) * ns),
            "rr_uniform": bf(np.random.uniform(size=H))}


def reference(x1, x2, W1, b1, W2, b2, noise_std, rr_uniform):
    out1 = (mxq(f64(x1), 1, "e4m3") @ mxq(f64(W1), 0, "e4m3")) + f64(b1)
    one_norm = np.sum(np.abs(out1), axis=1)
    sensitivity = np.max(one_norm) - np.min(one_norm)
    noise_mul = sensitivity / EPS
    out1 = out1 + f64(noise_std) * noise_mul
    rr_mask = np.where(f64(rr_uniform) < P_KEEP, 1.0, 0.0)
    out1 = out1 * rr_mask
    out2 = (mxq(f64(x2), 1, "e4m3") @ mxq(f64(W2), 0, "e4m3")) + f64(b2)
    return np.minimum(out1, out2)

@@ -1,0 +1,323 @@
+from contextlib import ExitStack
+
+import concourse.mybir as mybir
+from concourse.masks import make_identity
+
+F32 = mybir.dt.float32
+BF16 = mybir.dt.bfloat16
+U32 = mybir.dt.uint32
+U8 = mybir.dt.uint8
+FP8X4 = mybir.dt.float8_e4m3fn_x4
+ALU = mybir.AluOpType
+AX = mybir.AxisListType
+ACT = mybir.ActivationFunctionType
+
+P = 128
+B, F, H = 4096, 1024, 128
+T_ALL = B // P
+T_CH = 4
+N_CH = T_ALL // T_CH
+INV_EPS = 7.5
+P_KEEP = 0.95
+
+FLOPS = 2 * 2 * B * F * H
+
+
+def tile_splitnn_pa_t_kernel(tc, x1, x2, W1, b1, W2, b2, noise_std, rr_uniform, out):
+    nc = tc.nc
+    with ExitStack() as ctx:
+        const = ctx.enter_context(tc.tile_pool(name="const", bufs=1))
+        xpool = ctx.enter_context(tc.tile_pool(name="xpool", bufs=2 * N_CH))
+        gpool = ctx.enter_context(tc.tile_pool(name="gpool", bufs=3))
+        qpool = ctx.enter_context(tc.tile_pool(name="qpool", bufs=3))
+        opool = ctx.enter_context(tc.tile_pool(name="opool", bufs=3))
+        tpsum = ctx.enter_context(tc.psum_pool(name="tpsum", bufs=5))
+        apsum = ctx.enter_context(tc.psum_pool(name="apsum", bufs=3))
+
+        brow = const.tile([P, 512], BF16)
+        ones = const.tile([P, 256], BF16)
+        nc.vector.memset(brow[:], 0.0)
+        nc.vector.memset(ones[:], 1.0)
+        wraws = []
+
+        def load_w(wi, W):
+            wraw = const.tile([P, 1024], BF16, name="wraw%d" % wi)
+            nc.sync.dma_start(
+                out=wraw[:].rearrange("p (g r) -> p g r", g=2),
+                in_=W.rearrange("(g q t) h -> q g (t h)", g=2, q=P, t=4),
+            )
+            wraws.append(wraw)
+
+        xs = []
+        nz = const.tile([P, T_ALL * H], BF16)
+        for xi, x in enumerate((x1, x2)):
+            xv = x.rearrange("(p t) k -> p t k", t=T_ALL)
+            for c in range(N_CH):
+                x_sb = xpool.tile([P, T_CH * F], BF16, tag="x", name="x%d_%d" % (xi, c))
+                pieces = 4 if (xi == 0 and c < 2) else 1
+                tp_ = T_CH // pieces
+                for q in range(pieces):
+                    nc.sync.dma_start(
+                        out=x_sb[:, q * tp_ * F : (q + 1) * tp_ * F],
+                        in_=xv[:, c * T_CH + q * tp_ : c * T_CH + (q + 1) * tp_, :].rearrange("p t k -> p (t k)"),
+                    )
+                xs.append(x_sb)
+                if xi == 0 and c == 0:
+                    nc.sync.dma_start(out=brow[0:1, 0:128], in_=b1.rearrange("(o h) -> o h", o=1))
+                    nc.sync.dma_start(out=brow[0:1, 128:256], in_=b2.rearrange("(o h) -> o h", o=1))
+                    nc.sync.dma_start(out=brow[0:1, 256:384], in_=rr_uniform.rearrange("(o h) -> o h", o=1))
+                    load_w(0, W1)
+                if xi == 0 and c == 2:
+                    load_w(1, W2)
+                if xi == 0 and c == 5:
+                    nc.sync.dma_start(out=nz[:], in_=noise_std.rearrange("(p t) h -> p (t h)", t=T_ALL))
+        out_v = out.rearrange("(p t) h -> p t h", t=T_ALL)
+
+        ident = const.tile([P, P], F32)
+        make_identity(nc, ident[:])
+        b1f = const.tile([P, H], F32)
+        keep = const.tile([P, H], F32)
+        keep16 = const.tile([P, H], BF16)
+        b2col = const.tile([P, 1], F32)
+        b1_b = b1f[:].unsqueeze(1).to_broadcast([P, T_CH, H])
+        keep_b = keep[:].unsqueeze(1).to_broadcast([P, T_CH, H])
+
+        def spread_vectors():
+            bc_ps = apsum.tile([P, 512], F32, tag="acc", name="bc_ps")
+            nc.tensor.matmul(out=bc_ps[:], lhsT=ones[:, 0:P], rhs=brow[:], start=True, stop=True)
+            b2_ps = apsum.tile([P, 512], F32, tag="acc", name="b2_ps")
+            nc.tensor.matmul(out=b2_ps[:, 0:256], lhsT=brow[:, 128:256], rhs=ones[:], start=True, stop=True)
+            nc.vector.tensor_copy(out=b1f[:], in_=bc_ps[:, 0:128])
+            nc.vector.tensor_single_scalar(out=keep[:], in_=bc_ps[:, 256:384], scalar=P_KEEP, op=ALU.is_lt)
+            nc.vector.tensor_single_scalar(out=keep16[:], in_=bc_ps[:, 256:384], scalar=P_KEEP, op=ALU.is_lt)
+            nc.vector.tensor_copy(out=b2col[:], in_=b2_ps[:, 0:1])
+
+        wcs = []
+
+        def prepare_w(wi):
+            wg = const.tile([P, 1024], BF16, name="wg%d" % wi, align_bytes=64)
+            nc.vector.tensor_copy(
+                out=wg[:].rearrange("p (g h t) -> p g h t", g=2, h=H, t=4),
+                in_=wraws[wi][:].rearrange("p (g t h) -> p g h t", g=2, t=4, h=H),
+            )
+            wc = const.tile([P, 256], U32, name="wc%d" % wi, align_bytes=64)
+            ws = const.tile([P, 256], U8, name="ws%d" % wi, align_bytes=64)
+            wcs.append((wg, wc, ws))
+
+        def quantise_w(wi):
+            wg, wc, ws = wcs[wi]
+            nc.vector.quantize_mx(out=wc[:].bitcast(FP8X4), scales=ws[:], in_=wg[:])
+
+        a_all = const.tile([P, T_ALL * H], F32)
+        nrm = const.tile([P, T_ALL], F32)
+        mm = const.tile([P, 2], F32)
+        rep = const.tile([P, 256], F32)
+        gm = const.tile([P, 2], F32)
+        mul = const.tile([P, 1], F32)
+
+        banks = {}
+        grps = {}
+        codes = {}
+        accs = {}
+        absd = {}
+        dts = {}
+        dns = {}
+
+        def transposes(i, which):
+            xw = xs[i][:].bitcast(F32)
+            for bk in which:
+                bank = tpsum.tile([P, 512], F32, tag="tp", name="tp%d_%d" % (i, bk))
+                for s in range(4):
+                    if i < N_CH:
+                        t, g, u = bk, s // 2, s % 2
+                    else:
+                        t, g, u = 2 * (bk % 2) + s // 2, bk // 2, s % 2
+                    col = t * 512 + g * 256
+                    nc.tensor.transpose(bank[:, s * P : (s + 1) * P], xw[:, col + u : col + 256 : 2], ident[:])
+                banks[(i, bk)] = bank
+
+        def evacuate(i, bk, on_vector):
+            if i not in grps:
+                grps[i] = gpool.tile([P, T_CH * F], BF16, tag="grp", name="grp%d" % i, align_bytes=64)
+            gw = grps[i][:].bitcast(F32)
+            dst = gw[:, bk * 512 : (bk + 1) * 512].rearrange("p (g r u) -> p g r u", g=2, r=P, u=2)
+            src = banks[(i, bk)][:].rearrange("p (g u r) -> p g r u", g=2, u=2, r=P)
+            if on_vector:
+                nc.vector.tensor_copy(out=dst, in_=src)
+            else:
+                nc.scalar.copy(out=dst, in_=src)
+
+        def quantise(i):
+            cd = qpool.tile([P, T_CH * 256], U32, tag="cd", name="cd%d" % i, align_bytes=64)
+            sc = qpool.tile([P, T_CH * 256], U8, tag="sc", name="sc%d" % i, align_bytes=64)
+            nc.vector.quantize_mx(out=cd[:].bitcast(FP8X4), scales=sc[:], in_=grps[i][:])
+            codes[i] = (cd, sc)
+
+        def multiply(i):
+            cd, sc = codes[i]
+            wg, wc, ws = wcs[i // N_CH]
+            acc = apsum.tile([P, 512], F32, tag="acc", name="acc%d" % i)
+            if i < N_CH:
+                for t in range(T_CH):
+                    for g in range(2):
+                        col = (2 * t + g) * P
+                        nc.tensor.matmul_mx(
+                            out=acc[:, t * H : (t + 1) * H],
+                            lhsT=cd[:, col : col + P].bitcast(FP8X4),
+                            lhsT_scale=sc[:, col : col + P],
+                            rhs=wc[:, g * H : (g + 1) * H].bitcast(FP8X4),
+                            rhs_scale=ws[:, g * H : (g + 1) * H],
+                            start=(g == 0),
+                            stop=(g == 1),
+                        )
+            else:
+                for g in range(2):
+                    nc.tensor.matmul_mx(
+                        out=acc[:],
+                        lhsT=wc[:, g * H : (g + 1) * H].bitcast(FP8X4),
+                        lhsT_scale=ws[:, g * H : (g + 1) * H],
+                        rhs=cd[:, g * 512 : (g + 1) * 512].bitcast(FP8X4),
+                        rhs_scale=sc[:, g * 512 : (g + 1) * 512],
+                        start=(g == 0),
+                        stop=(g == 1),
+                    )
+            accs[i] = acc
+
+        def three(ap):
+            return ap.rearrange("p (t h) -> p t h", t=T_CH)
+
+        def a_chunk(c):
+            return a_all[:, c * 512 : (c + 1) * 512]
+
+        def add_b1(c):
+            nc.vector.tensor_tensor(out=three(a_chunk(c)), in0=three(accs[c][:]), in1=b1_b, op=ALU.add)
+
+        def absolute(c):
+            ab = opool.tile([P, 512], F32, tag="ab", name="ab%d" % c)
+            nc.scalar.activation(out=ab[:], in_=a_chunk(c), func=ACT.Abs)
+            absd[c] = ab
+
+        def norms(c):
+            nc.vector.tensor_reduce(
+                out=nrm[:, c * T_CH : (c + 1) * T_CH], in_=three(absd[c][:]), axis=AX.X, op=ALU.add
+            )
+
+        def spread_a():
+            nc.vector.tensor_reduce(out=mm[:, 0:1], in_=nrm[:], axis=AX.X, op=ALU.max)
+            nc.vector.tensor_reduce(out=mm[:, 1:2], in_=nrm[:], axis=AX.X, op=ALU.min)
+            nc.vector.tensor_copy(
+                out=rep[:].rearrange("p (s j) -> p s j", s=2),
+                in_=mm[:].unsqueeze(2).to_broadcast([P, 2, P]),
+            )
+
+        def spread_b():
+            sp = tpsum.tile([P, 512], F32, tag="tp", name="sp")
+            nc.tensor.transpose(sp[:, 0:P], rep[:, 0:P], ident[:])
+            nc.tensor.transpose(sp[:, P : 2 * P], rep[:, P : 2 * P], ident[:])
+            return sp
+
+        def spread_c(sp):
+            nc.vector.tensor_reduce(out=gm[:, 0:1], in_=sp[:, 0:P], axis=AX.X, op=ALU.max)
+            nc.vector.tensor_reduce(out=gm[:, 1:2], in_=sp[:, P : 2 * P], axis=AX.X, op=ALU.min)
+            nc.vector.tensor_scalar(
+                out=mul[:],
+                in0=gm[:, 0:1],
+                scalar1=gm[:, 1:2],
+                scalar2=INV_EPS,
+                op0=ALU.subtract,
+                op1=ALU.mult,
+            )
+
+        def add_b2(c):
+            dt_ = opool.tile([P, 512], F32, tag="dt", name="dt%d" % c)
+            nc.scalar.activation(out=dt_[:], in_=accs[N_CH + c][:], func=ACT.Identity, bias=b2col[:, 0:1], scale=1.0)
+            dts[c] = dt_
+
+        def back(c):
+            dn = apsum.tile([P, 512], F32, tag="acc", name="dn%d" % c)
+            for t in range(T_CH):
+                nc.tensor.transpose(dn[:, t * P : (t + 1) * P], dts[c][:, t * P : (t + 1) * P], ident[:])
+            dns[c] = dn
+
+        def noisy(c):
+            a_c = a_chunk(c)
+            nc.vector.scalar_tensor_tensor(
+                out=a_c,
+                in0=nz[:, c * 512 : (c + 1) * 512],
+                scalar=mul[:, 0:1],
+                in1=a_c,
+                op0=ALU.mult,
+                op1=ALU.add,
+            )
+
+        def mask_a(c):
+            a_c = a_chunk(c)
+            nc.gpsimd.tensor_tensor(out=three(a_c), in0=three(a_c), in1=keep_b, op=ALU.mult)
+
+        def mask_noise(q):
+            n_q = nz[:, q * 1024 : (q + 1) * 1024].rearrange("p (t h) -> p t h", t=2 * T_CH)
+            nc.vector.tensor_tensor(
+                out=n_q, in0=n_q, in1=keep16[:].unsqueeze(1).to_broadcast([P, 2 * T_CH, H]), op=ALU.mult
+            )
+
+        def minimum(c):
+            o = opool.tile([P, 512], F32, tag="o", name="o%d" % c)
+            nc.vector.tensor_tensor(out=o[:], in0=dns[c][:], in1=a_chunk(c), op=ALU.min)
+            nc.sync.dma_start(out=out_v[:, c * T_CH : (c + 1) * T_CH, :], in_=three(o[:]))
+
+        def on_vector(i, bk):
+            return i < N_CH and bk == 3 and i % 2 == 1
+
+        n_all = 2 * N_CH
+        sp = None
+        for i in range(n_all + 4):
+            if i < n_all:
+                transposes(i, (0, 1, 2, 3))
+            if i == 0:
+                spread_vectors()
+                prepare_w(0)
+            if 0 <= i - N_CH - 4 < N_CH:
+                back(i - N_CH - 4)
+            if i == N_CH + 3:
+                sp = spread_b()
+            if 0 <= i - 2 < n_all:
+                multiply(i - 2)
+            if i < n_all:
+                for bk in range(4):
+                    if on_vector(i, bk):
+                        evacuate(i, bk, True)
+                mine = [bk for bk in range(4) if not on_vector(i, bk)]
+            else:
+                mine = []
+            for bk in mine[:2]:
+                evacuate(i, bk, False)
+            if 0 <= i - 3 < N_CH:
+                absolute(i - 3)
+            if 0 <= i - N_CH - 3 < N_CH:
+                add_b2(i - N_CH - 3)
+            for bk in mine[2:]:
+                evacuate(i, bk, False)
+            if 0 <= i - 3 < N_CH:
+                mask_a(i - 3)
+            if i == 0:
+                quantise_w(0)
+            if i == 3:
+                prepare_w(1)
+            if i == N_CH + 3:
+                spread_c(sp)
+            if 1 <= i <= n_all:
+                quantise(i - 1)
+            if i == 3:
+                quantise_w(1)
+            if 0 <= i - N_CH - 4 < N_CH:
+                minimum(i - N_CH - 4)
+            if 0 <= i - N_CH - 3 < N_CH:
+                noisy(i - N_CH - 3)
+            if 0 <= i - 2 < N_CH:
+                add_b1(i - 2)
+            if 0 <= i - 3 < N_CH:
+                norms(i - 3)
+                if i - 3 == N_CH - 1:
+                    spread_a()
+            if 0 <= i - N_CH < 4:
+                mask_noise(i - N_CH)

@@ -119,7 +119,6 @@ def tile_splitnn_pa_t_kernel(tc, x1, x2, W1, b1, W2, b2, noise_std, rr_uniform, 
         grps = {}
         codes = {}
         accs = {}
-        absd = {}
         dts = {}
         dns = {}
 
@@ -192,14 +191,13 @@ def tile_splitnn_pa_t_kernel(tc, x1, x2, W1, b1, W2, b2, noise_std, rr_uniform, 
         def add_b1(c):
             nc.vector.tensor_tensor(out=three(a_chunk(c)), in0=three(accs[c][:]), in1=b1_b, op=ALU.add)
 
-        def absolute(c):
-            ab = opool.tile([P, 512], F32, tag="ab", name="ab%d" % c)
-            nc.scalar.activation(out=ab[:], in_=a_chunk(c), func=ACT.Abs)
-            absd[c] = ab
-
         def norms(c):
             nc.vector.tensor_reduce(
-                out=nrm[:, c * T_CH : (c + 1) * T_CH], in_=three(absd[c][:]), axis=AX.X, op=ALU.add
+                out=nrm[:, c * T_CH : (c + 1) * T_CH],
+                in_=three(a_chunk(c)),
+                axis=AX.X,
+                op=ALU.add,
+                apply_absolute_value=True,
             )
 
         def spread_a():
@@ -265,9 +263,6 @@ def tile_splitnn_pa_t_kernel(tc, x1, x2, W1, b1, W2, b2, noise_std, rr_uniform, 
             nc.vector.tensor_tensor(out=o[:], in0=dns[c][:], in1=a_chunk(c), op=ALU.min)
             nc.sync.dma_start(out=out_v[:, c * T_CH : (c + 1) * T_CH, :], in_=three(o[:]))
 
-        def on_vector(i, bk):
-            return i < N_CH and bk == 3 and i % 2 == 1
-
         n_all = 2 * N_CH
         sp = None
         for i in range(n_all + 4):
@@ -282,23 +277,13 @@ def tile_splitnn_pa_t_kernel(tc, x1, x2, W1, b1, W2, b2, noise_std, rr_uniform, 
                 sp = spread_b()
             if 0 <= i - 2 < n_all:
                 multiply(i - 2)
-            if i < n_all:
-                for bk in range(4):
-                    if on_vector(i, bk):
-                        evacuate(i, bk, True)
-                mine = [bk for bk in range(4) if not on_vector(i, bk)]
-            else:
-                mine = []
+            mine = range(4) if i < n_all else ()
             for bk in mine[:2]:
                 evacuate(i, bk, False)
-            if 0 <= i - 3 < N_CH:
-                absolute(i - 3)
             if 0 <= i - N_CH - 3 < N_CH:
                 add_b2(i - N_CH - 3)
             for bk in mine[2:]:
                 evacuate(i, bk, False)
-            if 0 <= i - 3 < N_CH:
-                mask_a(i - 3)
             if i == 0:
                 quantise_w(0)
             if i == 3:
@@ -317,6 +302,7 @@ def tile_splitnn_pa_t_kernel(tc, x1, x2, W1, b1, W2, b2, noise_std, rr_uniform, 
                 add_b1(i - 2)
             if 0 <= i - 3 < N_CH:
                 norms(i - 3)
+                mask_a(i - 3)
                 if i - 3 == N_CH - 1:
                     spread_a()
             if 0 <= i - N_CH < 4:

@@ -34,6 +34,8 @@ def tile_splitnn_pa_t_kernel(tc, x1, x2, W1, b1, W2, b2, noise_std, rr_uniform, 
         tpsum = ctx.enter_context(tc.psum_pool(name="tpsum", bufs=5))
         apsum = ctx.enter_context(tc.psum_pool(name="apsum", bufs=3))
 
+        ctx.enter_context(tc.manual_schedule())
+
         brow = const.tile([P, 512], BF16)
         ones = const.tile([P, 256], BF16)
         nc.vector.memset(brow[:], 0.0)
@@ -63,11 +65,11 @@ def tile_splitnn_pa_t_kernel(tc, x1, x2, W1, b1, W2, b2, noise_std, rr_uniform, 
                     )
                 xs.append(x_sb)
                 if xi == 0 and c == 0:
+                    load_w(0, W1)
                     nc.sync.dma_start(out=brow[0:1, 0:128], in_=b1.rearrange("(o h) -> o h", o=1))
                     nc.sync.dma_start(out=brow[0:1, 128:256], in_=b2.rearrange("(o h) -> o h", o=1))
                     nc.sync.dma_start(out=brow[0:1, 256:384], in_=rr_uniform.rearrange("(o h) -> o h", o=1))
-                    load_w(0, W1)
-                if xi == 0 and c == 2:
+                if xi == 0 and c == 1:
                     load_w(1, W2)
                 if xi == 0 and c == 5:
                     nc.sync.dma_start(out=nz[:], in_=noise_std.rearrange("(p t) h -> p (t h)", t=T_ALL))
@@ -77,7 +79,6 @@ def tile_splitnn_pa_t_kernel(tc, x1, x2, W1, b1, W2, b2, noise_std, rr_uniform, 
         make_identity(nc, ident[:])
         b1f = const.tile([P, H], F32)
         keep = const.tile([P, H], F32)
-        keep16 = const.tile([P, H], BF16)
         b2col = const.tile([P, 1], F32)
         b1_b = b1f[:].unsqueeze(1).to_broadcast([P, T_CH, H])
         keep_b = keep[:].unsqueeze(1).to_broadcast([P, T_CH, H])
@@ -87,9 +88,11 @@ def tile_splitnn_pa_t_kernel(tc, x1, x2, W1, b1, W2, b2, noise_std, rr_uniform, 
             nc.tensor.matmul(out=bc_ps[:], lhsT=ones[:, 0:P], rhs=brow[:], start=True, stop=True)
             b2_ps = apsum.tile([P, 512], F32, tag="acc", name="b2_ps")
             nc.tensor.matmul(out=b2_ps[:, 0:256], lhsT=brow[:, 128:256], rhs=ones[:], start=True, stop=True)
+            return bc_ps, b2_ps
+
+        def take_vectors(bc_ps, b2_ps):
             nc.vector.tensor_copy(out=b1f[:], in_=bc_ps[:, 0:128])
             nc.vector.tensor_single_scalar(out=keep[:], in_=bc_ps[:, 256:384], scalar=P_KEEP, op=ALU.is_lt)
-            nc.vector.tensor_single_scalar(out=keep16[:], in_=bc_ps[:, 256:384], scalar=P_KEEP, op=ALU.is_lt)
             nc.vector.tensor_copy(out=b2col[:], in_=b2_ps[:, 0:1])
 
         wcs = []
@@ -250,13 +253,7 @@ def tile_splitnn_pa_t_kernel(tc, x1, x2, W1, b1, W2, b2, noise_std, rr_uniform, 
 
         def mask_a(c):
             a_c = a_chunk(c)
-            nc.gpsimd.tensor_tensor(out=three(a_c), in0=three(a_c), in1=keep_b, op=ALU.mult)
-
-        def mask_noise(q):
-            n_q = nz[:, q * 1024 : (q + 1) * 1024].rearrange("p (t h) -> p t h", t=2 * T_CH)
-            nc.vector.tensor_tensor(
-                out=n_q, in0=n_q, in1=keep16[:].unsqueeze(1).to_broadcast([P, 2 * T_CH, H]), op=ALU.mult
-            )
+            nc.vector.tensor_tensor(out=three(a_c), in0=three(a_c), in1=keep_b, op=ALU.mult)
 
         def minimum(c):
             o = opool.tile([P, 512], F32, tag="o", name="o%d" % c)
@@ -264,46 +261,47 @@ def tile_splitnn_pa_t_kernel(tc, x1, x2, W1, b1, W2, b2, noise_std, rr_uniform, 
             nc.sync.dma_start(out=out_v[:, c * T_CH : (c + 1) * T_CH, :], in_=three(o[:]))
 
         n_all = 2 * N_CH
-        sp = None
         for i in range(n_all + 4):
             if i < n_all:
                 transposes(i, (0, 1, 2, 3))
-            if i == 0:
-                spread_vectors()
-                prepare_w(0)
             if 0 <= i - N_CH - 4 < N_CH:
                 back(i - N_CH - 4)
+            if i == 1:
+                vectors = spread_vectors()
             if i == N_CH + 3:
                 sp = spread_b()
             if 0 <= i - 2 < n_all:
                 multiply(i - 2)
-            mine = range(4) if i < n_all else ()
-            for bk in mine[:2]:
-                evacuate(i, bk, False)
+            if i < n_all:
+                evacuate(i, 0, False)
+                evacuate(i, 1, False)
             if 0 <= i - N_CH - 3 < N_CH:
                 add_b2(i - N_CH - 3)
-            for bk in mine[2:]:
-                evacuate(i, bk, False)
+            if i < n_all:
+                evacuate(i, 2, False)
+                evacuate(i, 3, False)
+            if 0 <= i - N_CH - 4 < N_CH:
+                mask_a(i - N_CH - 4)
             if i == 0:
+                prepare_w(0)
                 quantise_w(0)
-            if i == 3:
+            if i == 2:
                 prepare_w(1)
-            if i == N_CH + 3:
-                spread_c(sp)
+            if 0 <= i - 3 < N_CH:
+                add_b1(i - 3)
             if 1 <= i <= n_all:
                 quantise(i - 1)
-            if i == 3:
+            if i == 1:
+                take_vectors(*vectors)
+            if i == 2:
                 quantise_w(1)
+            if 0 <= i - 3 < N_CH:
+                norms(i - 3)
+            if i == N_CH + 2:
+                spread_a()
+            if i == N_CH + 3:
+                spread_c(sp)
             if 0 <= i - N_CH - 4 < N_CH:
                 minimum(i - N_CH - 4)
             if 0 <= i - N_CH - 3 < N_CH:
                 noisy(i - N_CH - 3)
-            if 0 <= i - 2 < N_CH:
-                add_b1(i - 2)
-            if 0 <= i - 3 < N_CH:
-                norms(i - 3)
-                mask_a(i - 3)
-                if i - 3 == N_CH - 1:
-                    spread_a()
-            if 0 <= i - N_CH < 4:
-                mask_noise(i - N_CH)

@@ -31,6 +31,7 @@ def tile_splitnn_pa_t_kernel(tc, x1, x2, W1, b1, W2, b2, noise_std, rr_uniform, 
         gpool = ctx.enter_context(tc.tile_pool(name="gpool", bufs=3))
         qpool = ctx.enter_context(tc.tile_pool(name="qpool", bufs=3))
         opool = ctx.enter_context(tc.tile_pool(name="opool", bufs=3))
+        spool = ctx.enter_context(tc.tile_pool(name="spool", bufs=6))
         tpsum = ctx.enter_context(tc.psum_pool(name="tpsum", bufs=5))
         apsum = ctx.enter_context(tc.psum_pool(name="apsum", bufs=3))
 
@@ -56,7 +57,7 @@ def tile_splitnn_pa_t_kernel(tc, x1, x2, W1, b1, W2, b2, noise_std, rr_uniform, 
             xv = x.rearrange("(p t) k -> p t k", t=T_ALL)
             for c in range(N_CH):
                 x_sb = xpool.tile([P, T_CH * F], BF16, tag="x", name="x%d_%d" % (xi, c))
-                pieces = 4 if (xi == 0 and c < 2) else 1
+                pieces = 4 if (xi == 0 and c < 4) else 1
                 tp_ = T_CH // pieces
                 for q in range(pieces):
                     nc.sync.dma_start(
@@ -64,14 +65,14 @@ def tile_splitnn_pa_t_kernel(tc, x1, x2, W1, b1, W2, b2, noise_std, rr_uniform, 
                         in_=xv[:, c * T_CH + q * tp_ : c * T_CH + (q + 1) * tp_, :].rearrange("p t k -> p (t k)"),
                     )
                 xs.append(x_sb)
-                if xi == 0 and c == 0:
+                if xi == 0 and c == 1:
                     load_w(0, W1)
                     nc.sync.dma_start(out=brow[0:1, 0:128], in_=b1.rearrange("(o h) -> o h", o=1))
                     nc.sync.dma_start(out=brow[0:1, 128:256], in_=b2.rearrange("(o h) -> o h", o=1))
                     nc.sync.dma_start(out=brow[0:1, 256:384], in_=rr_uniform.rearrange("(o h) -> o h", o=1))
-                if xi == 0 and c == 1:
+                if xi == 0 and c == 3:
                     load_w(1, W2)
-                if xi == 0 and c == 5:
+                if xi == 0 and c == 7:
                     nc.sync.dma_start(out=nz[:], in_=noise_std.rearrange("(p t) h -> p (t h)", t=T_ALL))
         out_v = out.rearrange("(p t) h -> p t h", t=T_ALL)
 
@@ -79,6 +80,7 @@ def tile_splitnn_pa_t_kernel(tc, x1, x2, W1, b1, W2, b2, noise_std, rr_uniform, 
         make_identity(nc, ident[:])
         b1f = const.tile([P, H], F32)
         keep = const.tile([P, H], F32)
+        keep16 = const.tile([P, H], BF16)
         b2col = const.tile([P, 1], F32)
         b1_b = b1f[:].unsqueeze(1).to_broadcast([P, T_CH, H])
         keep_b = keep[:].unsqueeze(1).to_broadcast([P, T_CH, H])
@@ -93,6 +95,7 @@ def tile_splitnn_pa_t_kernel(tc, x1, x2, W1, b1, W2, b2, noise_std, rr_uniform, 
         def take_vectors(bc_ps, b2_ps):
             nc.vector.tensor_copy(out=b1f[:], in_=bc_ps[:, 0:128])
             nc.vector.tensor_single_scalar(out=keep[:], in_=bc_ps[:, 256:384], scalar=P_KEEP, op=ALU.is_lt)
+            nc.vector.tensor_single_scalar(out=keep16[:], in_=bc_ps[:, 256:384], scalar=P_KEEP, op=ALU.is_lt)
             nc.vector.tensor_copy(out=b2col[:], in_=b2_ps[:, 0:1])
 
         wcs = []
@@ -133,7 +136,7 @@ def tile_splitnn_pa_t_kernel(tc, x1, x2, W1, b1, W2, b2, noise_std, rr_uniform, 
                     if i < N_CH:
                         t, g, u = bk, s // 2, s % 2
                     else:
-                        t, g, u = 2 * (bk % 2) + s // 2, bk // 2, s % 2
+                        t, g, u = 2 * (bk // 2) + s // 2, bk % 2, s % 2
                     col = t * 512 + g * 256
                     nc.tensor.transpose(bank[:, s * P : (s + 1) * P], xw[:, col + u : col + 256 : 2], ident[:])
                 banks[(i, bk)] = bank
@@ -149,41 +152,52 @@ def tile_splitnn_pa_t_kernel(tc, x1, x2, W1, b1, W2, b2, noise_std, rr_uniform, 
             else:
                 nc.scalar.copy(out=dst, in_=src)
 
-        def quantise(i):
-            cd = qpool.tile([P, T_CH * 256], U32, tag="cd", name="cd%d" % i, align_bytes=64)
-            sc = qpool.tile([P, T_CH * 256], U8, tag="sc", name="sc%d" % i, align_bytes=64)
-            nc.vector.quantize_mx(out=cd[:].bitcast(FP8X4), scales=sc[:], in_=grps[i][:])
-            codes[i] = (cd, sc)
-
-        def multiply(i):
+        def quantise(i, halves=(0, 1)):
+            if i not in codes:
+                cd = qpool.tile([P, T_CH * 256], U32, tag="cd", name="cd%d" % i, align_bytes=64)
+                sc = qpool.tile([P, T_CH * 256], U8, tag="sc", name="sc%d" % i, align_bytes=64)
+                codes[i] = (cd, sc)
             cd, sc = codes[i]
-            wg, wc, ws = wcs[i // N_CH]
+            lo, hi = halves[0] * 512, (halves[-1] + 1) * 512
+            nc.vector.quantize_mx(
+                out=cd[:, lo:hi].bitcast(FP8X4), scales=sc[:, lo:hi], in_=grps[i][:, 4 * lo : 4 * hi]
+            )
+
+        def multiply1(i):
+            cd, sc = codes[i]
+            wg, wc, ws = wcs[0]
             acc = apsum.tile([P, 512], F32, tag="acc", name="acc%d" % i)
-            if i < N_CH:
-                for t in range(T_CH):
-                    for g in range(2):
-                        col = (2 * t + g) * P
-                        nc.tensor.matmul_mx(
-                            out=acc[:, t * H : (t + 1) * H],
-                            lhsT=cd[:, col : col + P].bitcast(FP8X4),
-                            lhsT_scale=sc[:, col : col + P],
-                            rhs=wc[:, g * H : (g + 1) * H].bitcast(FP8X4),
-                            rhs_scale=ws[:, g * H : (g + 1) * H],
-                            start=(g == 0),
-                            stop=(g == 1),
-                        )
-            else:
+            for t in range(T_CH):
                 for g in range(2):
+                    col = (2 * t + g) * P
                     nc.tensor.matmul_mx(
-                        out=acc[:],
-                        lhsT=wc[:, g * H : (g + 1) * H].bitcast(FP8X4),
-                        lhsT_scale=ws[:, g * H : (g + 1) * H],
-                        rhs=cd[:, g * 512 : (g + 1) * 512].bitcast(FP8X4),
-                        rhs_scale=sc[:, g * 512 : (g + 1) * 512],
+                        out=acc[:, t * H : (t + 1) * H],
+                        lhsT=cd[:, col : col + P].bitcast(FP8X4),
+                        lhsT_scale=sc[:, col : col + P],
+                        rhs=wc[:, g * H : (g + 1) * H].bitcast(FP8X4),
+                        rhs_scale=ws[:, g * H : (g + 1) * H],
                         start=(g == 0),
                         stop=(g == 1),
                     )
             accs[i] = acc
+
+        def multiply2(i, halves=(0, 1)):
+            cd, sc = codes[i]
+            wg, wc, ws = wcs[1]
+            acc = apsum.tile([P, 512], F32, tag="acc", name="acc%d_%d" % (i, halves[0]))
+            for th in halves:
+                for g in range(2):
+                    col = (2 * th + g) * 256
+                    nc.tensor.matmul_mx(
+                        out=acc[:, th * 256 : (th + 1) * 256],
+                        lhsT=wc[:, g * H : (g + 1) * H].bitcast(FP8X4),
+                        lhsT_scale=ws[:, g * H : (g + 1) * H],
+                        rhs=cd[:, col : col + 256].bitcast(FP8X4),
+                        rhs_scale=sc[:, col : col + 256],
+                        start=(g == 0),
+                        stop=(g == 1),
+                    )
+                accs[(i, th)] = acc
 
         def three(ap):
             return ap.rearrange("p (t h) -> p t h", t=T_CH)
@@ -229,16 +243,27 @@ def tile_splitnn_pa_t_kernel(tc, x1, x2, W1, b1, W2, b2, noise_std, rr_uniform, 
                 op1=ALU.mult,
             )
 
-        def add_b2(c):
-            dt_ = opool.tile([P, 512], F32, tag="dt", name="dt%d" % c)
-            nc.scalar.activation(out=dt_[:], in_=accs[N_CH + c][:], func=ACT.Identity, bias=b2col[:, 0:1], scale=1.0)
-            dts[c] = dt_
+        def add_b2(c, halves=(0, 1)):
+            lo, hi = halves[0] * 256, (halves[-1] + 1) * 256
+            dt_ = opool.tile([P, 512], F32, tag="dt", name="dt%d_%d" % (c, halves[0]))
+            nc.scalar.activation(
+                out=dt_[:, lo:hi],
+                in_=accs[(N_CH + c, halves[0])][:, lo:hi],
+                func=ACT.Identity,
+                bias=b2col[:, 0:1],
+                scale=1.0,
+            )
+            for th in halves:
+                dts[(c, th)] = dt_
 
-        def back(c):
-            dn = apsum.tile([P, 512], F32, tag="acc", name="dn%d" % c)
-            for t in range(T_CH):
-                nc.tensor.transpose(dn[:, t * P : (t + 1) * P], dts[c][:, t * P : (t + 1) * P], ident[:])
-            dns[c] = dn
+        def back(c, halves=(0, 1), pool=apsum, tag="acc"):
+            dn = pool.tile([P, 512], F32, tag=tag, name="dn%d_%d" % (c, halves[0]))
+            for th in halves:
+                for t in (2 * th, 2 * th + 1):
+                    nc.tensor.transpose(
+                        dn[:, t * P : (t + 1) * P], dts[(c, th)][:, t * P : (t + 1) * P], ident[:]
+                    )
+                dns[(c, th)] = dn
 
         def noisy(c):
             a_c = a_chunk(c)
@@ -253,55 +278,91 @@ def tile_splitnn_pa_t_kernel(tc, x1, x2, W1, b1, W2, b2, noise_std, rr_uniform, 
 
         def mask_a(c):
             a_c = a_chunk(c)
-            nc.vector.tensor_tensor(out=three(a_c), in0=three(a_c), in1=keep_b, op=ALU.mult)
+            nc.gpsimd.tensor_tensor(out=three(a_c), in0=three(a_c), in1=keep_b, op=ALU.mult)
 
-        def minimum(c):
-            o = opool.tile([P, 512], F32, tag="o", name="o%d" % c)
-            nc.vector.tensor_tensor(out=o[:], in0=dns[c][:], in1=a_chunk(c), op=ALU.min)
-            nc.sync.dma_start(out=out_v[:, c * T_CH : (c + 1) * T_CH, :], in_=three(o[:]))
+        def mask_noise(q):
+            n_q = nz[:, q * 1024 : (q + 1) * 1024].rearrange("p (t h) -> p t h", t=2 * T_CH)
+            nc.vector.tensor_tensor(
+                out=n_q, in0=n_q, in1=keep16[:].unsqueeze(1).to_broadcast([P, 2 * T_CH, H]), op=ALU.mult
+            )
+
+        def minimum(c, halves=(0, 1)):
+            lo, hi = halves[0] * 256, (halves[-1] + 1) * 256
+            o = spool.tile([P, 512], F32, tag="o", name="o%d_%d" % (c, halves[0]))
+            nc.vector.tensor_tensor(
+                out=o[:, lo:hi], in0=dns[(c, halves[0])][:, lo:hi], in1=a_chunk(c)[:, lo:hi], op=ALU.min
+            )
+            t0, t1 = c * T_CH + lo // H, c * T_CH + hi // H
+            nc.sync.dma_start(
+                out=out_v[:, t0:t1, :], in_=o[:, lo:hi].rearrange("p (t h) -> p t h", t=t1 - t0)
+            )
 
         n_all = 2 * N_CH
-        for i in range(n_all + 4):
-            if i < n_all:
-                transposes(i, (0, 1, 2, 3))
-            if 0 <= i - N_CH - 4 < N_CH:
-                back(i - N_CH - 4)
-            if i == 1:
+        for i in range(n_all):
+            if 0 <= i - 4 < N_CH:
+                norms(i - 4)
+                mask_a(i - 4)
+            if i == N_CH + 3:
+                spread_a()
+            transposes(i, (0, 1, 2, 3))
+            if i == 2:
                 vectors = spread_vectors()
+            if i >= N_CH + 4:
+                back(i - N_CH - 4)
             if i == N_CH + 3:
                 sp = spread_b()
-            if 0 <= i - 2 < n_all:
-                multiply(i - 2)
-            if i < n_all:
-                evacuate(i, 0, False)
-                evacuate(i, 1, False)
-            if 0 <= i - N_CH - 3 < N_CH:
+            evacuate(i, 0, False)
+            evacuate(i, 1, False)
+            if i >= N_CH + 3:
                 add_b2(i - N_CH - 3)
-            if i < n_all:
-                evacuate(i, 2, False)
+            evacuate(i, 2, False)
+            if i < n_all - 1:
                 evacuate(i, 3, False)
-            if 0 <= i - N_CH - 4 < N_CH:
-                mask_a(i - N_CH - 4)
-            if i == 0:
+            if i == 2:
                 prepare_w(0)
                 quantise_w(0)
-            if i == 2:
+            if i == 3:
                 prepare_w(1)
-            if 0 <= i - 3 < N_CH:
-                add_b1(i - 3)
-            if 1 <= i <= n_all:
+            if 1 <= i:
                 quantise(i - 1)
-            if i == 1:
-                take_vectors(*vectors)
             if i == 2:
+                take_vectors(*vectors)
+            if i == 3:
                 quantise_w(1)
             if 0 <= i - 3 < N_CH:
-                norms(i - 3)
-            if i == N_CH + 2:
-                spread_a()
+                add_b1(i - 3)
+            if 0 <= i - N_CH + 1 < 4:
+                mask_noise(i - N_CH + 1)
             if i == N_CH + 3:
                 spread_c(sp)
-            if 0 <= i - N_CH - 4 < N_CH:
+            if i >= N_CH + 4:
                 minimum(i - N_CH - 4)
-            if 0 <= i - N_CH - 3 < N_CH:
-                noisy(i - N_CH - 3)
+            if 0 <= i - N_CH - 3 < 4:
+                noisy(2 * (i - N_CH - 3))
+                noisy(2 * (i - N_CH - 3) + 1)
+            if 2 <= i < N_CH + 2:
+                multiply1(i - 2)
+            elif i >= N_CH + 2:
+                multiply2(i - 2)
+        last = n_all - 1
+        tail = {"pool": tpsum, "tag": "tp"}
+        quantise(last, (0,))
+        evacuate(last, 3, True)
+        multiply2(last - 1)
+        back(4)
+        add_b2(5)
+        minimum(4)
+        quantise(last, (1,))
+        multiply2(last, (0,))
+        back(5, **tail)
+        add_b2(6)
+        minimum(5)
+        back(6, **tail)
+        add_b2(7, (0,))
+        multiply2(last, (1,))
+        minimum(6)
+        back(7, (0,), **tail)
+        add_b2(7, (1,))
+        minimum(7, (0,))
+        back(7, (1,), **tail)
+        minimum(7, (1,))

@@ -278,7 +278,7 @@ def tile_splitnn_pa_t_kernel(tc, x1, x2, W1, b1, W2, b2, noise_std, rr_uniform, 
 
         def mask_a(c):
             a_c = a_chunk(c)
-            nc.gpsimd.tensor_tensor(out=three(a_c), in0=three(a_c), in1=keep_b, op=ALU.mult)
+            nc.vector.tensor_tensor(out=three(a_c), in0=three(a_c), in1=keep_b, op=ALU.mult)
 
         def mask_noise(q):
             n_q = nz[:, q * 1024 : (q + 1) * 1024].rearrange("p (t h) -> p t h", t=2 * T_CH)
@@ -301,7 +301,6 @@ def tile_splitnn_pa_t_kernel(tc, x1, x2, W1, b1, W2, b2, noise_std, rr_uniform, 
         for i in range(n_all):
             if 0 <= i - 4 < N_CH:
                 norms(i - 4)
-                mask_a(i - 4)
             if i == N_CH + 3:
                 spread_a()
             transposes(i, (0, 1, 2, 3))
@@ -331,6 +330,8 @@ def tile_splitnn_pa_t_kernel(tc, x1, x2, W1, b1, W2, b2, noise_std, rr_uniform, 
                 quantise_w(1)
             if 0 <= i - 3 < N_CH:
                 add_b1(i - 3)
+            if 0 <= i - 4 < N_CH:
+                mask_a(i - 4)
             if 0 <= i - N_CH + 1 < 4:
                 mask_noise(i - N_CH + 1)
             if i == N_CH + 3:

@@ -217,6 +217,17 @@ def tile_splitnn_pa_t_kernel(tc, x1, x2, W1, b1, W2, b2, noise_std, rr_uniform, 
                 apply_absolute_value=True,
             )
 
+        def norms_on_scalar(c, blocks):
+            ab = opool.tile([P, 256], F32, tag="ab", name="ab%d_%d" % (c, blocks[0]))
+            for j, t in enumerate(blocks):
+                col = c * T_CH + t
+                nc.scalar.activation(
+                    out=ab[:, j * H : (j + 1) * H],
+                    in_=a_all[:, col * H : (col + 1) * H],
+                    func=ACT.Abs,
+                    accum_out=nrm[:, col : col + 1],
+                )
+
         def spread_a():
             nc.vector.tensor_reduce(out=mm[:, 0:1], in_=nrm[:], axis=AX.X, op=ALU.max)
             nc.vector.tensor_reduce(out=mm[:, 1:2], in_=nrm[:], axis=AX.X, op=ALU.min)
@@ -234,6 +245,8 @@ def tile_splitnn_pa_t_kernel(tc, x1, x2, W1, b1, W2, b2, noise_std, rr_uniform, 
         def spread_c(sp):
             nc.vector.tensor_reduce(out=gm[:, 0:1], in_=sp[:, 0:P], axis=AX.X, op=ALU.max)
             nc.vector.tensor_reduce(out=gm[:, 1:2], in_=sp[:, P : 2 * P], axis=AX.X, op=ALU.min)
+
+        def spread_d():
             nc.vector.tensor_scalar(
                 out=mul[:],
                 in0=gm[:, 0:1],
@@ -299,7 +312,7 @@ def tile_splitnn_pa_t_kernel(tc, x1, x2, W1, b1, W2, b2, noise_std, rr_uniform, 
 
         n_all = 2 * N_CH
         for i in range(n_all):
-            if 0 <= i - 4 < N_CH:
+            if 0 <= i - 4 < N_CH and i % 2 == 1:
                 norms(i - 4)
             if i == N_CH + 3:
                 spread_a()
@@ -308,43 +321,48 @@ def tile_splitnn_pa_t_kernel(tc, x1, x2, W1, b1, W2, b2, noise_std, rr_uniform, 
                 vectors = spread_vectors()
             if i >= N_CH + 4:
                 back(i - N_CH - 4)
-            if i == N_CH + 3:
-                sp = spread_b()
             evacuate(i, 0, False)
             evacuate(i, 1, False)
+            if 0 <= i - 4 < N_CH and i % 2 == 0:
+                norms_on_scalar(i - 4, (0, 1))
             if i >= N_CH + 3:
                 add_b2(i - N_CH - 3)
             evacuate(i, 2, False)
             if i < n_all - 1:
                 evacuate(i, 3, False)
+            if 0 <= i - 4 < N_CH and i % 2 == 0:
+                norms_on_scalar(i - 4, (2, 3))
             if i == 2:
                 prepare_w(0)
                 quantise_w(0)
-            if i == 3:
+            if i == 5:
                 prepare_w(1)
+            if i == N_CH + 4:
+                spread_c(sp)
             if 1 <= i:
                 quantise(i - 1)
             if i == 2:
                 take_vectors(*vectors)
-            if i == 3:
+            if i == 5:
                 quantise_w(1)
             if 0 <= i - 3 < N_CH:
                 add_b1(i - 3)
-            if 0 <= i - 4 < N_CH:
-                mask_a(i - 4)
-            if 0 <= i - N_CH + 1 < 4:
-                mask_noise(i - N_CH + 1)
-            if i == N_CH + 3:
-                spread_c(sp)
+            if 0 <= i - 5 < N_CH:
+                mask_a(i - 5)
+            if 0 <= i - N_CH < 4:
+                mask_noise(i - N_CH)
+            if i == N_CH + 4:
+                spread_d()
             if i >= N_CH + 4:
+                noisy(2 * (i - N_CH - 4))
+                noisy(2 * (i - N_CH - 4) + 1)
                 minimum(i - N_CH - 4)
-            if 0 <= i - N_CH - 3 < 4:
-                noisy(2 * (i - N_CH - 3))
-                noisy(2 * (i - N_CH - 3) + 1)
             if 2 <= i < N_CH + 2:
                 multiply1(i - 2)
             elif i >= N_CH + 2:
                 multiply2(i - 2)
+            if i == N_CH + 3:
+                sp = spread_b()
         last = n_all - 1
         tail = {"pool": tpsum, "tag": "tp"}
         quantise(last, (0,))

@@ -57,7 +57,7 @@ def tile_splitnn_pa_t_kernel(tc, x1, x2, W1, b1, W2, b2, noise_std, rr_uniform, 
             xv = x.rearrange("(p t) k -> p t k", t=T_ALL)
             for c in range(N_CH):
                 x_sb = xpool.tile([P, T_CH * F], BF16, tag="x", name="x%d_%d" % (xi, c))
-                pieces = 4 if (xi == 0 and c < 4) else 1
+                pieces = 4 if (xi == 0 and c < 6) else 1
                 tp_ = T_CH // pieces
                 for q in range(pieces):
                     nc.sync.dma_start(
@@ -70,9 +70,9 @@ def tile_splitnn_pa_t_kernel(tc, x1, x2, W1, b1, W2, b2, noise_std, rr_uniform, 
                     nc.sync.dma_start(out=brow[0:1, 0:128], in_=b1.rearrange("(o h) -> o h", o=1))
                     nc.sync.dma_start(out=brow[0:1, 128:256], in_=b2.rearrange("(o h) -> o h", o=1))
                     nc.sync.dma_start(out=brow[0:1, 256:384], in_=rr_uniform.rearrange("(o h) -> o h", o=1))
-                if xi == 0 and c == 3:
+                if xi == 0 and c == 5:
                     load_w(1, W2)
-                if xi == 0 and c == 7:
+                if xi == 0 and c == 6:
                     nc.sync.dma_start(out=nz[:], in_=noise_std.rearrange("(p t) h -> p (t h)", t=T_ALL))
         out_v = out.rearrange("(p t) h -> p t h", t=T_ALL)
 
@@ -83,7 +83,6 @@ def tile_splitnn_pa_t_kernel(tc, x1, x2, W1, b1, W2, b2, noise_std, rr_uniform, 
         keep16 = const.tile([P, H], BF16)
         b2col = const.tile([P, 1], F32)
         b1_b = b1f[:].unsqueeze(1).to_broadcast([P, T_CH, H])
-        keep_b = keep[:].unsqueeze(1).to_broadcast([P, T_CH, H])
 
         def spread_vectors():
             bc_ps = apsum.tile([P, 512], F32, tag="acc", name="bc_ps")
@@ -208,7 +207,7 @@ def tile_splitnn_pa_t_kernel(tc, x1, x2, W1, b1, W2, b2, noise_std, rr_uniform, 
         def add_b1(c):
             nc.vector.tensor_tensor(out=three(a_chunk(c)), in0=three(accs[c][:]), in1=b1_b, op=ALU.add)
 
-        def norms(c):
+        def norms_on_vector(c):
             nc.vector.tensor_reduce(
                 out=nrm[:, c * T_CH : (c + 1) * T_CH],
                 in_=three(a_chunk(c)),
@@ -278,20 +277,21 @@ def tile_splitnn_pa_t_kernel(tc, x1, x2, W1, b1, W2, b2, noise_std, rr_uniform, 
                     )
                 dns[(c, th)] = dn
 
-        def noisy(c):
-            a_c = a_chunk(c)
+        def noisy(q):
+            two = slice(q * 1024, (q + 1) * 1024)
             nc.vector.scalar_tensor_tensor(
-                out=a_c,
-                in0=nz[:, c * 512 : (c + 1) * 512],
+                out=a_all[:, two],
+                in0=nz[:, two],
                 scalar=mul[:, 0:1],
-                in1=a_c,
+                in1=a_all[:, two],
                 op0=ALU.mult,
                 op1=ALU.add,
             )
 
-        def mask_a(c):
-            a_c = a_chunk(c)
-            nc.vector.tensor_tensor(out=three(a_c), in0=three(a_c), in1=keep_b, op=ALU.mult)
+        def mask_a(c, n=1):
+            a_c = a_all[:, c * 512 : (c + n) * 512].rearrange("p (t h) -> p t h", h=H)
+            keep_b = keep[:].unsqueeze(1).to_broadcast([P, n * T_CH, H])
+            nc.vector.tensor_tensor(out=a_c, in0=a_c, in1=keep_b, op=ALU.mult)
 
         def mask_noise(q):
             n_q = nz[:, q * 1024 : (q + 1) * 1024].rearrange("p (t h) -> p t h", t=2 * T_CH)
@@ -311,74 +311,74 @@ def tile_splitnn_pa_t_kernel(tc, x1, x2, W1, b1, W2, b2, noise_std, rr_uniform, 
             )
 
         n_all = 2 * N_CH
+        bar = N_CH + 3
         for i in range(n_all):
-            if 0 <= i - 4 < N_CH and i % 2 == 1:
-                norms(i - 4)
-            if i == N_CH + 3:
-                spread_a()
-            transposes(i, (0, 1, 2, 3))
+            if 0 <= i - 3 < N_CH:
+                add_b1(i - 3)
+            transposes(i, (0, 1))
+            if i == bar:
+                sp = spread_b()
+            transposes(i, (2, 3))
             if i == 2:
                 vectors = spread_vectors()
-            if i >= N_CH + 4:
-                back(i - N_CH - 4)
+            if i > bar:
+                back(i - bar - 1)
             evacuate(i, 0, False)
             evacuate(i, 1, False)
-            if 0 <= i - 4 < N_CH and i % 2 == 0:
-                norms_on_scalar(i - 4, (0, 1))
-            if i >= N_CH + 3:
-                add_b2(i - N_CH - 3)
+            if 3 <= i < bar - 1:
+                norms_on_scalar(i - 3, (0, 1))
+            if i >= bar:
+                add_b2(i - bar)
             evacuate(i, 2, False)
-            if i < n_all - 1:
-                evacuate(i, 3, False)
-            if 0 <= i - 4 < N_CH and i % 2 == 0:
-                norms_on_scalar(i - 4, (2, 3))
+            evacuate(i, 3, False)
+            if 3 <= i < bar - 1:
+                norms_on_scalar(i - 3, (2, 3))
             if i == 2:
                 prepare_w(0)
                 quantise_w(0)
-            if i == 5:
+            if i == 7:
                 prepare_w(1)
-            if i == N_CH + 4:
-                spread_c(sp)
             if 1 <= i:
                 quantise(i - 1)
             if i == 2:
                 take_vectors(*vectors)
-            if i == 5:
+            if i == 7:
                 quantise_w(1)
-            if 0 <= i - 3 < N_CH:
-                add_b1(i - 3)
-            if 0 <= i - 5 < N_CH:
-                mask_a(i - 5)
-            if 0 <= i - N_CH < 4:
-                mask_noise(i - N_CH)
-            if i == N_CH + 4:
+            if i == bar - 1:
+                norms_on_vector(N_CH - 1)
+            if i == bar:
+                spread_c(sp)
+            if 0 <= i - 4 < N_CH:
+                mask_a(i - 4)
+            if i == bar - 1:
+                spread_a()
+            if i == bar:
                 spread_d()
-            if i >= N_CH + 4:
-                noisy(2 * (i - N_CH - 4))
-                noisy(2 * (i - N_CH - 4) + 1)
-                minimum(i - N_CH - 4)
+            if 0 <= i - bar + 4 < 4:
+                mask_noise(i - bar + 4)
+            if bar <= i < bar + 4:
+                noisy(i - bar)
+            if i > bar:
+                minimum(i - bar - 1)
             if 2 <= i < N_CH + 2:
                 multiply1(i - 2)
             elif i >= N_CH + 2:
                 multiply2(i - 2)
-            if i == N_CH + 3:
-                sp = spread_b()
         last = n_all - 1
         tail = {"pool": tpsum, "tag": "tp"}
         quantise(last, (0,))
-        evacuate(last, 3, True)
+        quantise(last, (1,))
         multiply2(last - 1)
         back(4)
         add_b2(5)
         minimum(4)
-        quantise(last, (1,))
         multiply2(last, (0,))
         back(5, **tail)
         add_b2(6)
         minimum(5)
-        back(6, **tail)
         add_b2(7, (0,))
         multiply2(last, (1,))
+        back(6, **tail)
         minimum(6)
         back(7, (0,), **tail)
         add_b2(7, (1,))

@@ -162,11 +162,13 @@ def tile_splitnn_pa_t_kernel(tc, x1, x2, W1, b1, W2, b2, noise_std, rr_uniform, 
                 out=cd[:, lo:hi].bitcast(FP8X4), scales=sc[:, lo:hi], in_=grps[i][:, 4 * lo : 4 * hi]
             )
 
-        def multiply1(i):
+        def multiply1(i, th):
             cd, sc = codes[i]
             wg, wc, ws = wcs[0]
-            acc = apsum.tile([P, 512], F32, tag="acc", name="acc%d" % i)
-            for t in range(T_CH):
+            if i not in accs:
+                accs[i] = apsum.tile([P, 512], F32, tag="acc", name="acc%d" % i)
+            acc = accs[i]
+            for t in (2 * th, 2 * th + 1):
                 for g in range(2):
                     col = (2 * t + g) * P
                     nc.tensor.matmul_mx(
@@ -178,12 +180,12 @@ def tile_splitnn_pa_t_kernel(tc, x1, x2, W1, b1, W2, b2, noise_std, rr_uniform, 
                         start=(g == 0),
                         stop=(g == 1),
                     )
-            accs[i] = acc
 
-        def multiply2(i, halves=(0, 1)):
+        def multiply2(i, halves, acc=None):
             cd, sc = codes[i]
             wg, wc, ws = wcs[1]
-            acc = apsum.tile([P, 512], F32, tag="acc", name="acc%d_%d" % (i, halves[0]))
+            if acc is None:
+                acc = apsum.tile([P, 512], F32, tag="acc", name="acc%d_%d" % (i, halves[0]))
             for th in halves:
                 for g in range(2):
                     col = (2 * th + g) * 256
@@ -318,6 +320,10 @@ def tile_splitnn_pa_t_kernel(tc, x1, x2, W1, b1, W2, b2, noise_std, rr_uniform, 
             transposes(i, (0, 1))
             if i == bar:
                 sp = spread_b()
+            if 3 <= i < N_CH + 2:
+                multiply1(i - 2, 0)
+            elif i >= N_CH + 2:
+                multiply2(i - 2, (0,))
             transposes(i, (2, 3))
             if i == 2:
                 vectors = spread_vectors()
@@ -360,15 +366,17 @@ def tile_splitnn_pa_t_kernel(tc, x1, x2, W1, b1, W2, b2, noise_std, rr_uniform, 
                 noisy(i - bar)
             if i > bar:
                 minimum(i - bar - 1)
+            if i == 2:
+                multiply1(0, 0)
             if 2 <= i < N_CH + 2:
-                multiply1(i - 2)
+                multiply1(i - 2, 1)
             elif i >= N_CH + 2:
-                multiply2(i - 2)
+                multiply2(i - 2, (1,), accs[(i - 2, 0)])
         last = n_all - 1
         tail = {"pool": tpsum, "tag": "tp"}
         quantise(last, (0,))
         quantise(last, (1,))
-        multiply2(last - 1)
+        multiply2(last - 1, (0, 1))
         back(4)
         add_b2(5)
         minimum(4)

@@ -30,6 +30,7 @@ def tile_splitnn_pa_t_kernel(tc, x1, x2, W1, b1, W2, b2, noise_std, rr_uniform, 
         xpool = ctx.enter_context(tc.tile_pool(name="xpool", bufs=2 * N_CH))
         gpool = ctx.enter_context(tc.tile_pool(name="gpool", bufs=3))
         qpool = ctx.enter_context(tc.tile_pool(name="qpool", bufs=3))
+        wpool = ctx.enter_context(tc.tile_pool(name="wpool", bufs=2))
         opool = ctx.enter_context(tc.tile_pool(name="opool", bufs=3))
         spool = ctx.enter_context(tc.tile_pool(name="spool", bufs=6))
         tpsum = ctx.enter_context(tc.psum_pool(name="tpsum", bufs=5))
@@ -70,10 +71,14 @@ def tile_splitnn_pa_t_kernel(tc, x1, x2, W1, b1, W2, b2, noise_std, rr_uniform, 
                     nc.sync.dma_start(out=brow[0:1, 0:128], in_=b1.rearrange("(o h) -> o h", o=1))
                     nc.sync.dma_start(out=brow[0:1, 128:256], in_=b2.rearrange("(o h) -> o h", o=1))
                     nc.sync.dma_start(out=brow[0:1, 256:384], in_=rr_uniform.rearrange("(o h) -> o h", o=1))
-                if xi == 0 and c == 5:
+                if xi == 0 and c == 3:
                     load_w(1, W2)
-                if xi == 0 and c == 6:
-                    nc.sync.dma_start(out=nz[:], in_=noise_std.rearrange("(p t) h -> p (t h)", t=T_ALL))
+                q = xi * N_CH + c - 5
+                if 0 <= q < 4:
+                    nc.sync.dma_start(
+                        out=nz[:, q * 1024 : (q + 1) * 1024],
+                        in_=noise_std.rearrange("(p t) h -> p (t h)", t=T_ALL)[:, q * 1024 : (q + 1) * 1024],
+                    )
         out_v = out.rearrange("(p t) h -> p t h", t=T_ALL)
 
         ident = const.tile([P, P], F32)
@@ -127,6 +132,18 @@ def tile_splitnn_pa_t_kernel(tc, x1, x2, W1, b1, W2, b2, noise_std, rr_uniform, 
         dts = {}
         dns = {}
 
+        words = {}
+
+        def order_words(i, bk):
+            th, g = bk // 2, bk % 2
+            ordered = wpool.tile([P, 512], F32, tag="ordered", name="ordered%d_%d" % (i, bk))
+            half = xs[i][:].bitcast(F32)[:, th * 1024 : (th + 1) * 1024]
+            nc.scalar.copy(
+                out=ordered[:].rearrange("p (b u m) -> p b u m", b=2, u=2),
+                in_=half.rearrange("p (b c m u) -> p b c u m", b=2, c=2, u=2)[:, :, g],
+            )
+            words[(i, bk)] = ordered
+
         def transposes(i, which):
             xw = xs[i][:].bitcast(F32)
             for bk in which:
@@ -137,7 +154,10 @@ def tile_splitnn_pa_t_kernel(tc, x1, x2, W1, b1, W2, b2, noise_std, rr_uniform, 
                     else:
                         t, g, u = 2 * (bk // 2) + s // 2, bk % 2, s % 2
                     col = t * 512 + g * 256
-                    nc.tensor.transpose(bank[:, s * P : (s + 1) * P], xw[:, col + u : col + 256 : 2], ident[:])
+                    src = xw[:, col + u : col + 256 : 2]
+                    if (i, bk) in words:
+                        src = words[(i, bk)][:, s * P : (s + 1) * P]
+                    nc.tensor.transpose(bank[:, s * P : (s + 1) * P], src, ident[:])
                 banks[(i, bk)] = bank
 
         def evacuate(i, bk, on_vector):
@@ -315,41 +335,47 @@ def tile_splitnn_pa_t_kernel(tc, x1, x2, W1, b1, W2, b2, noise_std, rr_uniform, 
         n_all = 2 * N_CH
         bar = N_CH + 3
         for i in range(n_all):
+            if i == 4:
+                prepare_w(1)
+                quantise_w(1)
             if 0 <= i - 3 < N_CH:
                 add_b1(i - 3)
             transposes(i, (0, 1))
-            if i == bar:
-                sp = spread_b()
             if 3 <= i < N_CH + 2:
                 multiply1(i - 2, 0)
             elif i >= N_CH + 2:
                 multiply2(i - 2, (0,))
             transposes(i, (2, 3))
+            if i == bar:
+                sp = spread_b()
             if i == 2:
                 vectors = spread_vectors()
-            if i > bar:
+            if bar < i < n_all - 1:
                 back(i - bar - 1)
+            elif i == n_all - 1:
+                back(i - bar - 1, pool=tpsum, tag="tp")
             evacuate(i, 0, False)
             evacuate(i, 1, False)
             if 3 <= i < bar - 1:
                 norms_on_scalar(i - 3, (0, 1))
-            if i >= bar:
+            if bar <= i < n_all - 1:
                 add_b2(i - bar)
             evacuate(i, 2, False)
-            evacuate(i, 3, False)
+            if bar - 1 <= i < bar + 2:
+                order_words(i + 1, 3)
+            if i < n_all - 1:
+                evacuate(i, 3, False)
+            else:
+                add_b2(i - bar)
             if 3 <= i < bar - 1:
                 norms_on_scalar(i - 3, (2, 3))
             if i == 2:
                 prepare_w(0)
                 quantise_w(0)
-            if i == 7:
-                prepare_w(1)
             if 1 <= i:
                 quantise(i - 1)
             if i == 2:
                 take_vectors(*vectors)
-            if i == 7:
-                quantise_w(1)
             if i == bar - 1:
                 norms_on_vector(N_CH - 1)
             if i == bar:
@@ -364,7 +390,7 @@ def tile_splitnn_pa_t_kernel(tc, x1, x2, W1, b1, W2, b2, noise_std, rr_uniform, 
                 mask_noise(i - bar + 4)
             if bar <= i < bar + 4:
                 noisy(i - bar)
-            if i > bar:
+            if bar < i < n_all - 1:
                 minimum(i - bar - 1)
             if i == 2:
                 multiply1(0, 0)
@@ -374,11 +400,13 @@ def tile_splitnn_pa_t_kernel(tc, x1, x2, W1, b1, W2, b2, noise_std, rr_uniform, 
                 multiply2(i - 2, (1,), accs[(i - 2, 0)])
         last = n_all - 1
         tail = {"pool": tpsum, "tag": "tp"}
+        evacuate(last, 3, True)
         quantise(last, (0,))
         quantise(last, (1,))
         multiply2(last - 1, (0, 1))
-        back(4)
+        back(4, **tail)
         add_b2(5)
+        minimum(3)
         minimum(4)
         multiply2(last, (0,))
         back(5, **tail)

from contextlib import ExitStack

import concourse.mybir as mybir
from concourse.masks import make_identity

F32 = mybir.dt.float32
BF16 = mybir.dt.bfloat16
U32 = mybir.dt.uint32
U8 = mybir.dt.uint8
FP8X4 = mybir.dt.float8_e4m3fn_x4
ALU = mybir.AluOpType
AX = mybir.AxisListType
ACT = mybir.ActivationFunctionType

P = 128
B, F, H = 4096, 1024, 128
T_ALL = B // P
T_CH = 4
N_CH = T_ALL // T_CH
INV_EPS = 7.5
P_KEEP = 0.95

FLOPS = 2 * 2 * B * F * H


def tile_splitnn_pa_t_kernel(tc, x1, x2, W1, b1, W2, b2, noise_std, rr_uniform, out):
    nc = tc.nc
    with ExitStack() as ctx:
        const = ctx.enter_context(tc.tile_pool(name="const", bufs=1))
        xpool = ctx.enter_context(tc.tile_pool(name="xpool", bufs=2 * N_CH))
        gpool = ctx.enter_context(tc.tile_pool(name="gpool", bufs=3))
        qpool = ctx.enter_context(tc.tile_pool(name="qpool", bufs=3))
        wpool = ctx.enter_context(tc.tile_pool(name="wpool", bufs=2))
        opool = ctx.enter_context(tc.tile_pool(name="opool", bufs=3))
        spool = ctx.enter_context(tc.tile_pool(name="spool", bufs=6))
        tpsum = ctx.enter_context(tc.psum_pool(name="tpsum", bufs=5))
        apsum = ctx.enter_context(tc.psum_pool(name="apsum", bufs=3))

        ctx.enter_context(tc.manual_schedule())

        brow = const.tile([P, 512], BF16)
        ones = const.tile([P, 256], BF16)
        nc.vector.memset(brow[:], 0.0)
        nc.vector.memset(ones[:], 1.0)
        wraws = []

        def load_w(wi, W):
            wraw = const.tile([P, 1024], BF16, name="wraw%d" % wi)
            nc.sync.dma_start(
                out=wraw[:].rearrange("p (g r) -> p g r", g=2),
                in_=W.rearrange("(g q t) h -> q g (t h)", g=2, q=P, t=4),
            )
            wraws.append(wraw)

        xs = []
        nz = const.tile([P, T_ALL * H], BF16)
        for xi, x in enumerate((x1, x2)):
            xv = x.rearrange("(p t) k -> p t k", t=T_ALL)
            for c in range(N_CH):
                x_sb = xpool.tile([P, T_CH * F], BF16, tag="x", name="x%d_%d" % (xi, c))
                pieces = 4 if (xi == 0 and c < 6) else 1
                tp_ = T_CH // pieces
                for q in range(pieces):
                    nc.sync.dma_start(
                        out=x_sb[:, q * tp_ * F : (q + 1) * tp_ * F],
                        in_=xv[:, c * T_CH + q * tp_ : c * T_CH + (q + 1) * tp_, :].rearrange("p t k -> p (t k)"),
                    )
                xs.append(x_sb)
                if xi == 0 and c == 1:
                    load_w(0, W1)
                    nc.sync.dma_start(out=brow[0:1, 0:128], in_=b1.rearrange("(o h) -> o h", o=1))
                    nc.sync.dma_start(out=brow[0:1, 128:256], in_=b2.rearrange("(o h) -> o h", o=1))
                    nc.sync.dma_start(out=brow[0:1, 256:384], in_=rr_uniform.rearrange("(o h) -> o h", o=1))
                if xi == 0 and c == 3:
                    load_w(1, W2)
                q = xi * N_CH + c - 5
                if 0 <= q < 4:
                    nc.sync.dma_start(
                        out=nz[:, q * 1024 : (q + 1) * 1024],
                        in_=noise_std.rearrange("(p t) h -> p (t h)", t=T_ALL)[:, q * 1024 : (q + 1) * 1024],
                    )
        out_v = out.rearrange("(p t) h -> p t h", t=T_ALL)

        ident = const.tile([P, P], F32)
        make_identity(nc, ident[:])
        b1f = const.tile([P, H], F32)
        keep = const.tile([P, H], F32)
        keep16 = const.tile([P, H], BF16)
        b2col = const.tile([P, 1], F32)
        b1_b = b1f[:].unsqueeze(1).to_broadcast([P, T_CH, H])

        def spread_vectors():
            bc_ps = apsum.tile([P, 512], F32, tag="acc", name="bc_ps")
            nc.tensor.matmul(out=bc_ps[:], lhsT=ones[:, 0:P], rhs=brow[:], start=True, stop=True)
            b2_ps = apsum.tile([P, 512], F32, tag="acc", name="b2_ps")
            nc.tensor.matmul(out=b2_ps[:, 0:256], lhsT=brow[:, 128:256], rhs=ones[:], start=True, stop=True)
            return bc_ps, b2_ps

        def take_vectors(bc_ps, b2_ps):
            nc.vector.tensor_copy(out=b1f[:], in_=bc_ps[:, 0:128])
            nc.vector.tensor_single_scalar(out=keep[:], in_=bc_ps[:, 256:384], scalar=P_KEEP, op=ALU.is_lt)
            nc.vector.tensor_single_scalar(out=keep16[:], in_=bc_ps[:, 256:384], scalar=P_KEEP, op=ALU.is_lt)
            nc.vector.tensor_copy(out=b2col[:], in_=b2_ps[:, 0:1])

        wcs = []

        def prepare_w(wi):
            wg = const.tile([P, 1024], BF16, name="wg%d" % wi, align_bytes=64)
            nc.vector.tensor_copy(
                out=wg[:].rearrange("p (g h t) -> p g h t", g=2, h=H, t=4),
                in_=wraws[wi][:].rearrange("p (g t h) -> p g h t", g=2, t=4, h=H),
            )
            wc = const.tile([P, 256], U32, name="wc%d" % wi, align_bytes=64)
            ws = const.tile([P, 256], U8, name="ws%d" % wi, align_bytes=64)
            wcs.append((wg, wc, ws))

        def quantise_w(wi):
            wg, wc, ws = wcs[wi]
            nc.vector.quantize_mx(out=wc[:].bitcast(FP8X4), scales=ws[:], in_=wg[:])

        a_all = const.tile([P, T_ALL * H], F32)
        nrm = const.tile([P, T_ALL], F32)
        mm = const.tile([P, 2], F32)
        rep = const.tile([P, 256], F32)
        gm = const.tile([P, 2], F32)
        mul = const.tile([P, 1], F32)

        banks = {}
        grps = {}
        codes = {}
        accs = {}
        dts = {}
        dns = {}

        words = {}

        def order_words(i, bk):
            th, g = bk // 2, bk % 2
            ordered = wpool.tile([P, 512], F32, tag="ordered", name="ordered%d_%d" % (i, bk))
            half = xs[i][:].bitcast(F32)[:, th * 1024 : (th + 1) * 1024]
            nc.scalar.copy(
                out=ordered[:].rearrange("p (b u m) -> p b u m", b=2, u=2),
                in_=half.rearrange("p (b c m u) -> p b c u m", b=2, c=2, u=2)[:, :, g],
            )
            words[(i, bk)] = ordered

        def transposes(i, which):
            xw = xs[i][:].bitcast(F32)
            for bk in which:
                bank = tpsum.tile([P, 512], F32, tag="tp", name="tp%d_%d" % (i, bk))
                for s in range(4):
                    if i < N_CH:
                        t, g, u = bk, s // 2, s % 2
                    else:
                        t, g, u = 2 * (bk // 2) + s // 2, bk % 2, s % 2
                    col = t * 512 + g * 256
                    src = xw[:, col + u : col + 256 : 2]
                    if (i, bk) in words:
                        src = words[(i, bk)][:, s * P : (s + 1) * P]
                    nc.tensor.transpose(bank[:, s * P : (s + 1) * P], src, ident[:])
                banks[(i, bk)] = bank

        def evacuate(i, bk, on_vector):
            if i not in grps:
                grps[i] = gpool.tile([P, T_CH * F], BF16, tag="grp", name="grp%d" % i, align_bytes=64)
            gw = grps[i][:].bitcast(F32)
            dst = gw[:, bk * 512 : (bk + 1) * 512].rearrange("p (g r u) -> p g r u", g=2, r=P, u=2)
            src = banks[(i, bk)][:].rearrange("p (g u r) -> p g r u", g=2, u=2, r=P)
            if on_vector:
                nc.vector.tensor_copy(out=dst, in_=src)
            else:
                nc.scalar.copy(out=dst, in_=src)

        def quantise(i, halves=(0, 1)):
            if i not in codes:
                cd = qpool.tile([P, T_CH * 256], U32, tag="cd", name="cd%d" % i, align_bytes=64)
                sc = qpool.tile([P, T_CH * 256], U8, tag="sc", name="sc%d" % i, align_bytes=64)
                codes[i] = (cd, sc)
            cd, sc = codes[i]
            lo, hi = halves[0] * 512, (halves[-1] + 1) * 512
            nc.vector.quantize_mx(
                out=cd[:, lo:hi].bitcast(FP8X4), scales=sc[:, lo:hi], in_=grps[i][:, 4 * lo : 4 * hi]
            )

        def multiply1(i, th):
            cd, sc = codes[i]
            wg, wc, ws = wcs[0]
            if i not in accs:
                accs[i] = apsum.tile([P, 512], F32, tag="acc", name="acc%d" % i)
            acc = accs[i]
            for t in (2 * th, 2 * th + 1):
                for g in range(2):
                    col = (2 * t + g) * P
                    nc.tensor.matmul_mx(
                        out=acc[:, t * H : (t + 1) * H],
                        lhsT=cd[:, col : col + P].bitcast(FP8X4),
                        lhsT_scale=sc[:, col : col + P],
                        rhs=wc[:, g * H : (g + 1) * H].bitcast(FP8X4),
                        rhs_scale=ws[:, g * H : (g + 1) * H],
                        start=(g == 0),
                        stop=(g == 1),
                    )

        def multiply2(i, halves, acc=None):
            cd, sc = codes[i]
            wg, wc, ws = wcs[1]
            if acc is None:
                acc = apsum.tile([P, 512], F32, tag="acc", name="acc%d_%d" % (i, halves[0]))
            for th in halves:
                for g in range(2):
                    col = (2 * th + g) * 256
                    nc.tensor.matmul_mx(
                        out=acc[:, th * 256 : (th + 1) * 256],
                        lhsT=wc[:, g * H : (g + 1) * H].bitcast(FP8X4),
                        lhsT_scale=ws[:, g * H : (g + 1) * H],
                        rhs=cd[:, col : col + 256].bitcast(FP8X4),
                        rhs_scale=sc[:, col : col + 256],
                        start=(g == 0),
                        stop=(g == 1),
                    )
                accs[(i, th)] = acc

        def three(ap):
            return ap.rearrange("p (t h) -> p t h", t=T_CH)

        def a_chunk(c):
            return a_all[:, c * 512 : (c + 1) * 512]

        def add_b1(c):
            nc.vector.tensor_tensor(out=three(a_chunk(c)), in0=three(accs[c][:]), in1=b1_b, op=ALU.add)

        def norms_on_vector(c):
            nc.vector.tensor_reduce(
                out=nrm[:, c * T_CH : (c + 1) * T_CH],
                in_=three(a_chunk(c)),
                axis=AX.X,
                op=ALU.add,
                apply_absolute_value=True,
            )

        def norms_on_scalar(c, blocks):
            ab = opool.tile([P, 256], F32, tag="ab", name="ab%d_%d" % (c, blocks[0]))
            for j, t in enumerate(blocks):
                col = c * T_CH + t
                nc.scalar.activation(
                    out=ab[:, j * H : (j + 1) * H],
                    in_=a_all[:, col * H : (col + 1) * H],
                    func=ACT.Abs,
                    accum_out=nrm[:, col : col + 1],
                )

        def spread_a():
            nc.vector.tensor_reduce(out=mm[:, 0:1], in_=nrm[:], axis=AX.X, op=ALU.max)
            nc.vector.tensor_reduce(out=mm[:, 1:2], in_=nrm[:], axis=AX.X, op=ALU.min)
            nc.vector.tensor_copy(
                out=rep[:].rearrange("p (s j) -> p s j", s=2),
                in_=mm[:].unsqueeze(2).to_broadcast([P, 2, P]),
            )

        def spread_b():
            sp = tpsum.tile([P, 512], F32, tag="tp", name="sp")
            nc.tensor.transpose(sp[:, 0:P], rep[:, 0:P], ident[:])
            nc.tensor.transpose(sp[:, P : 2 * P], rep[:, P : 2 * P], ident[:])
            return sp

        def spread_c(sp):
            nc.vector.tensor_reduce(out=gm[:, 0:1], in_=sp[:, 0:P], axis=AX.X, op=ALU.max)
            nc.vector.tensor_reduce(out=gm[:, 1:2], in_=sp[:, P : 2 * P], axis=AX.X, op=ALU.min)

        def spread_d():
            nc.vector.tensor_scalar(
                out=mul[:],
                in0=gm[:, 0:1],
                scalar1=gm[:, 1:2],
                scalar2=INV_EPS,
                op0=ALU.subtract,
                op1=ALU.mult,
            )

        def add_b2(c, halves=(0, 1)):
            lo, hi = halves[0] * 256, (halves[-1] + 1) * 256
            dt_ = opool.tile([P, 512], F32, tag="dt", name="dt%d_%d" % (c, halves[0]))
            nc.scalar.activation(
                out=dt_[:, lo:hi],
                in_=accs[(N_CH + c, halves[0])][:, lo:hi],
                func=ACT.Identity,
                bias=b2col[:, 0:1],
                scale=1.0,
            )
            for th in halves:
                dts[(c, th)] = dt_

        def back(c, halves=(0, 1), pool=apsum, tag="acc"):
            dn = pool.tile([P, 512], F32, tag=tag, name="dn%d_%d" % (c, halves[0]))
            for th in halves:
                for t in (2 * th, 2 * th + 1):
                    nc.tensor.transpose(
                        dn[:, t * P : (t + 1) * P], dts[(c, th)][:, t * P : (t + 1) * P], ident[:]
                    )
                dns[(c, th)] = dn

        def noisy(q):
            two = slice(q * 1024, (q + 1) * 1024)
            nc.vector.scalar_tensor_tensor(
                out=a_all[:, two],
                in0=nz[:, two],
                scalar=mul[:, 0:1],
                in1=a_all[:, two],
                op0=ALU.mult,
                op1=ALU.add,
            )

        def mask_a(c, n=1):
            a_c = a_all[:, c * 512 : (c + n) * 512].rearrange("p (t h) -> p t h", h=H)
            keep_b = keep[:].unsqueeze(1).to_broadcast([P, n * T_CH, H])
            nc.vector.tensor_tensor(out=a_c, in0=a_c, in1=keep_b, op=ALU.mult)

        def mask_noise(q):
            n_q = nz[:, q * 1024 : (q + 1) * 1024].rearrange("p (t h) -> p t h", t=2 * T_CH)
            nc.vector.tensor_tensor(
                out=n_q, in0=n_q, in1=keep16[:].unsqueeze(1).to_broadcast([P, 2 * T_CH, H]), op=ALU.mult
            )

        def minimum(c, halves=(0, 1)):
            lo, hi = halves[0] * 256, (halves[-1] + 1) * 256
            o = spool.tile([P, 512], F32, tag="o", name="o%d_%d" % (c, halves[0]))
            nc.vector.tensor_tensor(
                out=o[:, lo:hi], in0=dns[(c, halves[0])][:, lo:hi], in1=a_chunk(c)[:, lo:hi], op=ALU.min
            )
            t0, t1 = c * T_CH + lo // H, c * T_CH + hi // H
            nc.sync.dma_start(
                out=out_v[:, t0:t1, :], in_=o[:, lo:hi].rearrange("p (t h) -> p t h", t=t1 - t0)
            )

        n_all = 2 * N_CH
        bar = N_CH + 3
        for i in range(n_all):
            if i == 4:
                prepare_w(1)
                quantise_w(1)
            if 0 <= i - 3 < N_CH:
                add_b1(i - 3)
            transposes(i, (0, 1))
            if 3 <= i < N_CH + 2:
                multiply1(i - 2, 0)
            elif i >= N_CH + 2:
                multiply2(i - 2, (0,))
            transposes(i, (2, 3))
            if i == bar:
                sp = spread_b()
            if i == 2:
                vectors = spread_vectors()
            if bar < i < n_all - 1:
                back(i - bar - 1)
            elif i == n_all - 1:
                back(i - bar - 1, pool=tpsum, tag="tp")
            evacuate(i, 0, False)
            evacuate(i, 1, False)
            if 3 <= i < bar - 1:
                norms_on_scalar(i - 3, (0, 1))
            if bar <= i < n_all - 1:
                add_b2(i - bar)
            evacuate(i, 2, False)
            if bar - 1 <= i < bar + 2:
                order_words(i + 1, 3)
            if i < n_all - 1:
                evacuate(i, 3, False)
            else:
                add_b2(i - bar)
            if 3 <= i < bar - 1:
                norms_on_scalar(i - 3, (2, 3))
            if i == 2:
                prepare_w(0)
                quantise_w(0)
            if 1 <= i:
                quantise(i - 1)
            if i == 2:
                take_vectors(*vectors)
            if i == bar - 1:
                norms_on_vector(N_CH - 1)
            if i == bar:
                spread_c(sp)
            if 0 <= i - 4 < N_CH:
                mask_a(i - 4)
            if i == bar - 1:
                spread_a()
            if i == bar:
                spread_d()
            if 0 <= i - bar + 4 < 4:
                mask_noise(i - bar + 4)
            if bar <= i < bar + 4:
                noisy(i - bar)
            if bar < i < n_all - 1:
                minimum(i - bar - 1)
            if i == 2:
                multiply1(0, 0)
            if 2 <= i < N_CH + 2:
                multiply1(i - 2, 1)
            elif i >= N_CH + 2:
                multiply2(i - 2, (1,), accs[(i - 2, 0)])
        last = n_all - 1
        tail = {"pool": tpsum, "tag": "tp"}
        evacuate(last, 3, True)
        quantise(last, (0,))
        quantise(last, (1,))
        multiply2(last - 1, (0, 1))
        back(4, **tail)
        add_b2(5)
        minimum(3)
        minimum(4)
        multiply2(last, (0,))
        back(5, **tail)
        add_b2(6)
        minimum(5)
        add_b2(7, (0,))
        multiply2(last, (1,))
        back(6, **tail)
        minimum(6)
        back(7, (0,), **tail)
        add_b2(7, (1,))
        minimum(7, (0,))
        back(7, (1,), **tail)
        minimum(7, (1,))
